import numpy as np
import ml_dtypes


def mxq(x, axis, fmt="e4m3"):
    dtype, down = {"e4m3": (ml_dtypes.float8_e4m3fn, 7), "e5m2": (ml_dtypes.float8_e5m2, 14)}[fmt]
    v = np.moveaxis(np.asarray(x, np.float32).astype(ml_dtypes.bfloat16).astype(np.float64), axis, -1)
    blocks = v.reshape(v.shape[:-1] + (-1, 32))
    amax = np.abs(blocks).max(-1, keepdims=True)
    byte = np.maximum(np.where(amax > 0, np.frexp(amax)[1] - 1 + 127, 0) - down, 1)
    scale = np.exp2(byte - 127.0)
    codes = (blocks / scale).astype(np.float32).astype(dtype).astype(np.float64)
    return np.moveaxis((codes * scale).reshape(v.shape), -1, axis)


WIDE = False


def mx_kscale(k):
    if not WIDE:
        return np.ones(k)
    levels = np.array([10, -10, 5, -5, 0])
    if k % 512:
        return np.exp2(np.random.permutation(np.resize(levels, k // 32))).repeat(32)
    a = np.empty((k // 512, 16))
    for p in range(k // 512):
        a[p, :8] = np.random.permutation(np.resize(levels, 8))
        for g in range(8):
            far = levels[np.abs(levels - a[p, g]) >= 10]
            a[p, g + 8] = far[np.random.randint(len(far))]
    return np.exp2(a.ravel()).repeat(32)


BF16 = ml_dtypes.bfloat16


def bf(x):
    return np.asarray(x, np.float32).astype(BF16)


def f64(x):
    return np.asarray(x).astype(np.float64)


B, S, K, D, H, KV, HD = 2, 16, 32, 2048, 8, 2, 128
HP = HD // 2


def rope(v, cos, sin):
    vr, vi = v[..., 0::2], v[..., 1::2]
    out_r = vr * cos - vi * sin
    out_i = vr * sin + vi * cos
    return np.stack([out_r, out_i], axis=-1).reshape(v.shape)


def draw0():
    s = mx_kscale(D)
    return {"x": bf(np.random.standard_normal((B, S, K, D)) * s),
            "freqs": bf(np.random.uniform(size=(S, K, HP)) * 2.0 * np.pi),
            "wq": bf(np.random.standard_normal((H * HD, D)) * 1.25 / np.sqrt(D) / s),
            "wk": bf(np.random.standard_normal((KV * HD, D)) * 1.25 / np.sqrt(D) / s),
            "wv": bf(np.random.standard_normal((KV * HD, D)) * 2.0 / np.sqrt(D) / s)}


def core(x, freqs, wq, wk, wv):
    xm = mxq(f64(x), 3, "e4m3")
    q = (xm @ mxq(f64(wq), 1, "e4m3").T).reshape(B, S, K, H, HD)
    k = (xm @ mxq(f64(wk), 1, "e4m3").T).reshape(B, S, K, KV, HD)
    v = (xm @ mxq(f64(wv), 1, "e4m3").T).reshape(B, S, K, KV, HD)
    cos = np.cos(f64(freqs))[None, :, :, None, :]
    sin = np.sin(f64(freqs))[None, :, :, None, :]
    return rope(q, cos, sin), rope(k, cos, sin), v


def e4m3fn_bytes(y):
    return np.clip(np.asarray(y, np.float64), -448.0, 448.0).astype(np.float32).astype(ml_dtypes.float8_e4m3fn).view(np.uint8)


def e4m3fn_values(b):
    return np.asarray(b, np.uint8).view(ml_dtypes.float8_e4m3fn).astype(np.float64)


def setup_inputs():
    d = draw0()
    x0 = np.asarray(d['x']).astype(np.float64)
    s = (np.max(np.abs(x0), axis=(0, 1, 2), keepdims=True) / 448.0).astype(np.float32)
    out = {}
    for k, v in d.items():
        if k == 'x':
            out['x_bytes'] = e4m3fn_bytes(x0 / s.astype(np.float64))
            out['x_scale'] = s
        else:
            out[k] = v
    return out


def reference(x_bytes, x_scale, freqs, wq, wk, wv):
    return core(e4m3fn_values(x_bytes) * x_scale.astype(np.float64), freqs, wq, wk, wv)

@@ -1,0 +1,296 @@
+import math
+from contextlib import ExitStack
+
+import concourse.mybir as mybir
+from concourse.masks import make_identity
+
+F32 = mybir.dt.float32
+BF16 = mybir.dt.bfloat16
+U8 = mybir.dt.uint8
+U32 = mybir.dt.uint32
+FP8 = mybir.dt.float8_e4m3fn
+FP8X4 = mybir.dt.float8_e4m3fn_x4
+ACT = mybir.ActivationFunctionType
+ALU = mybir.AluOpType
+
+P = 128
+TOK = 1024
+D = 2048
+NPASS = 4
+NM = TOK // P
+FLOPS = 2 * TOK * D * 1536
+
+
+def tile_attention_pa_kernel(tc, x_bytes, x_scale, freqs, wq, wk, wv, out_0, out_1, out_2):
+    nc = tc.nc
+    xb_d = x_bytes.flatten_outer_dims()
+    sc_d = x_scale.rearrange("a b c k -> (a b c k)")
+    fr_d = freqs.rearrange("s k i -> (s k) i").rearrange("(j p) i -> p j i", p=P)
+    q_d = out_0.rearrange("b s k h d -> (b s k) (h d)")
+    k_d = out_1.rearrange("b s k h d -> (b s k) (h d)")
+    v_d = out_2.rearrange("b s k h d -> (b s k) (h d)")
+
+    with ExitStack() as ctx:
+        ctx.enter_context(tc.manual_schedule())
+        const = ctx.enter_context(tc.tile_pool(name="const", bufs=1))
+        raw = ctx.enter_context(tc.tile_pool(name="raw", bufs=1))
+        wrp = ctx.enter_context(tc.tile_pool(name="wrp", bufs=8))
+        keep = ctx.enter_context(tc.tile_pool(name="keep", bufs=1))
+        xsp = ctx.enter_context(tc.tile_pool(name="xsp", bufs=4))
+        xgp = ctx.enter_context(tc.tile_pool(name="xgp", bufs=2))
+        wgp = ctx.enter_context(tc.tile_pool(name="wgp", bufs=2))
+        rp = ctx.enter_context(tc.tile_pool(name="rp", bufs=3))
+        op = ctx.enter_context(tc.tile_pool(name="op", bufs=3))
+        ptp = ctx.enter_context(tc.psum_pool(name="ptp", bufs=3))
+        accp = ctx.enter_context(tc.psum_pool(name="accp", bufs=5))
+
+        scl = const.tile([P, D], F32, name="scl")
+        s_cols = const.tile([P, NPASS, 4], F32, name="s_cols")
+        xb = [raw.tile([P, D], U8, name="xb%d" % m) for m in range(NM)]
+        wr = {}
+        fr = const.tile([P, 4, 64], BF16, name="fr")
+        zero = const.tile([P, 1], F32, name="zero")
+        warm = const.tile([P, 1], F32, name="warm")
+
+        def load_x(m):
+            nc.sync.dma_start(out=xb[m][:], in_=xb_d[P * m:P * (m + 1), :])
+
+        def load_w(t):
+            if t < 8:
+                src = wq[P * t:P * (t + 1), :]
+            elif t < 10:
+                src = wk[P * (t - 8):P * (t - 7), :]
+            else:
+                src = wv[P * (t - 10):P * (t - 9), :]
+            wr[t] = wrp.tile([P, D], BF16, name="wr")
+            nc.sync.dma_start(out=wr[t][:], in_=src)
+
+        nc.vector.memset(zero[:], 0.0)
+        idle = const.tile([P, 512], BF16, name="idle")
+        nc.vector.memset(idle[:], 0.0)
+
+        def keep_warm(count):
+            for i in range(count):
+                junk = accp.tile([P, 512], F32, name="acc")
+                nc.tensor.matmul(out=junk[:], lhsT=idle[:, 0:P], rhs=idle[:], start=True, stop=True)
+
+        nc.sync.dma_start(out=s_cols[:], in_=sc_d.rearrange("(g p t) -> p g t", p=P, t=4))
+        nc.scalar.dma_start(out=fr[:], in_=fr_d)
+        nc.scalar.activation(out=warm[:], in_=zero[:], func=ACT.Sin)
+        load_x(0)
+        load_w(0)
+        load_x(1)
+        load_w(1)
+        load_w(2)
+        load_x(2)
+        load_w(3)
+        load_x(3)
+        for t in range(4, 8):
+            load_w(t)
+        load_x(4)
+        load_x(5)
+
+        ident = const.tile([P, P], F32, name="ident")
+        make_identity(nc, ident[:])
+        keep_warm(5)
+
+        for g in range(NPASS):
+            pb = ptp.tile([P, 4, P], F32, name="pt")
+            for t in range(4):
+                nc.tensor.transpose(pb[:, t, :], s_cols[:, g, t:t + 1].to_broadcast([P, P]), ident[:])
+            nc.scalar.copy(out=scl[:, 512 * g:512 * (g + 1)].rearrange("p (r t) -> p r t", t=4),
+                           in_=pb[:].rearrange("p t r -> p r t"))
+
+        wrap = const.tile([P, 4, 64], F32, name="wrap")
+        carg = const.tile([P, 4, 64], F32, name="carg")
+        tab = const.tile([P, 4, 2, P], F32, name="tab")
+        nc.vector.tensor_scalar(out=wrap[:], in0=fr[:], scalar1=1.5 * math.pi, scalar2=2.0 * math.pi,
+                                op0=ALU.is_gt, op1=ALU.mult)
+        nc.vector.tensor_tensor(out=carg[:], in0=wrap[:], in1=fr[:], op=ALU.subtract)
+
+        def tables():
+            nc.scalar.activation(out=tab[:, :, 0, :].rearrange("p j (i e) -> p j i e", e=2),
+                                 in_=carg[:].unsqueeze(3).to_broadcast([P, 4, 64, 2]),
+                                 func=ACT.Sin, bias=0.5 * math.pi, scale=1.0)
+            tsin = tab[:, :, 1, :].rearrange("p j (i e) -> p j i e", e=2)
+            nc.scalar.activation(out=tsin[:, :, :, 0], in_=fr[:], func=ACT.Sin, bias=math.pi, scale=-1.0)
+            nc.scalar.activation(out=tsin[:, :, :, 1], in_=fr[:], func=ACT.Sin, bias=-math.pi, scale=1.0)
+
+        xc = [keep.tile([P, 2, 512], U32, name="xc%d" % i, align_bytes=64) for i in range(NM // 2)]
+        xsc = [keep.tile([P, 2, 512], U8, name="xsc%d" % i, align_bytes=64) for i in range(NM // 2)]
+        wc = [keep.tile([P, NPASS, 512], U32, name="wc%d" % c, align_bytes=64) for c in range(3)]
+        wsc = [keep.tile([P, NPASS, 512], U8, name="wsc%d" % c, align_bytes=64) for c in range(3)]
+
+        xs = {}
+        xg = {}
+        wg = {}
+
+        def widen(m, chunks):
+            xs[m] = xsp.tile([P, D], BF16, name="xs", align_bytes=64)
+            w = D // chunks
+            for i in range(chunks):
+                nc.vector.tensor_tensor(out=xs[m][:, w * i:w * (i + 1)],
+                                        in0=xb[m][:, w * i:w * (i + 1)].bitcast(FP8),
+                                        in1=scl[:, w * i:w * (i + 1)], op=ALU.mult)
+
+        def turn(src_tile, dst_words):
+            words = src_tile[:].bitcast(F32)
+            for h in range(2):
+                pt = ptp.tile([P, 2, 2, P], F32, name="pt")
+                for gg in range(2):
+                    g = 2 * h + gg
+                    for u in range(2):
+                        nc.tensor.transpose(pt[:, gg, u, :], words[:, 256 * g + u:256 * (g + 1):2], ident[:])
+                nc.scalar.copy(out=dst_words(h), in_=pt[:].rearrange("p g u r -> p g r u"))
+
+        def turn_x(m):
+            if m % 2 == 0:
+                xg[m // 2] = xgp.tile([P, 2, NPASS, P, 4], BF16, name="xg", align_bytes=64)
+            xw = xg[m // 2][:, m % 2, :, :, :].bitcast(F32)
+            turn(xs[m], lambda h: xw[:, 2 * h:2 * h + 2, :, :])
+
+        def quant_x(i):
+            nc.vector.quantize_mx(out=xc[i][:].rearrange("p a n -> p (a n)").bitcast(FP8X4),
+                                  scales=xsc[i][:].rearrange("p a n -> p (a n)"),
+                                  in_=xg[i][:].rearrange("p a g r t -> p (a g r t)"))
+
+        def turn_w(t):
+            c, w = t // 4, t % 4
+            if w == 0:
+                wg[c] = wgp.tile([P, NPASS, 512, 4], BF16, name="wg", align_bytes=64)
+            ww = wg[c][:].bitcast(F32)
+            turn(wr[t], lambda h: ww[:, 2 * h:2 * h + 2, P * w:P * (w + 1), :])
+
+        def quant_w(c):
+            for h in range(2):
+                gs = slice(2 * h, 2 * h + 2)
+                nc.vector.quantize_mx(out=wc[c][:, gs, :].rearrange("p g n -> p (g n)").bitcast(FP8X4),
+                                      scales=wsc[c][:, gs, :].rearrange("p g n -> p (g n)"),
+                                      in_=wg[c][:, gs, :, :].rearrange("p g n t -> p (g n t)"))
+
+        acc = {}
+
+        def mm(m, c):
+            acc[(m, c)] = accp.tile([P, 512], F32, name="acc")
+            for g in range(NPASS):
+                nc.tensor.matmul_mx(out=acc[(m, c)][:],
+                                    lhsT=xc[m // 2][:, m % 2, P * g:P * (g + 1)].bitcast(FP8X4),
+                                    lhsT_scale=xsc[m // 2][:, m % 2, P * g:P * (g + 1)],
+                                    rhs=wc[c][:, g, :].bitcast(FP8X4),
+                                    rhs_scale=wsc[c][:, g, :],
+                                    start=(g == 0), stop=(g == NPASS - 1))
+
+        tt = {}
+        oo = {}
+
+        def add_store(eng, m, lo, hi):
+            rows = slice(P * m, P * (m + 1))
+            eng.tensor_tensor(
+                out=oo[m][:, lo:hi].rearrange("p (n e) -> p n e", e=2),
+                in0=tt[m][:, 0, lo:hi].rearrange("p (n e) -> p n e", e=2),
+                in1=tt[m][:, 1, lo:hi].rearrange("p (n e) -> p n e", e=2)[:, :, ::-1],
+                op=ALU.add)
+            if lo < 1024:
+                nc.sync.dma_start(out=q_d[rows, lo:min(hi, 1024)], in_=oo[m][:, lo:min(hi, 1024)])
+            if hi > 1024:
+                nc.sync.dma_start(out=k_d[rows, :], in_=oo[m][:, 1024:1280])
+
+        def rope(m, c):
+            a = acc[(m, c)]
+            j = m % 4
+            nh = 4 if c < 2 else 2
+            n = nh * P
+            rows = slice(P * m, P * (m + 1))
+            if c == 0:
+                tt[m] = rp.tile([P, 2, 1280], F32, name="t")
+                oo[m] = op.tile([P, 1280], F32, name="o")
+            if c == 2:
+                ov = op.tile([P, 256], F32, name="ov")
+                nc.scalar.copy(out=ov[:], in_=a[:, 256:512])
+                nc.sync.dma_start(out=v_d[rows, :], in_=ov[:])
+            nc.vector.tensor_tensor(
+                out=tt[m][:, :, 512 * c:512 * c + n].rearrange("p r (h c) -> p r h c", c=P),
+                in0=tab[:, j, :, :].unsqueeze(2).to_broadcast([P, 2, nh, P]),
+                in1=a[:, 0:n].rearrange("p (h c) -> p h c", c=P).unsqueeze(1).to_broadcast([P, 2, nh, P]),
+                op=ALU.mult)
+            if m == NM - 1:
+                if c == 1:
+                    add_store(nc.vector, m, 0, 1024)
+                if c == 2:
+                    add_store(nc.vector, m, 1024, 1280)
+            elif c == 2:
+                add_store(nc.gpsimd, m, 0, 1280)
+
+        widen(0, 4)
+        turn_w(0)
+        keep_warm(1)
+        load_w(8)
+        turn_w(1)
+        keep_warm(1)
+        load_w(9)
+        widen(1, 1)
+        turn_x(0)
+        keep_warm(1)
+        turn_w(2)
+        keep_warm(1)
+        load_w(10)
+        turn_w(3)
+        keep_warm(1)
+        load_w(11)
+        load_x(6)
+        load_x(7)
+        widen(2, 1)
+        turn_x(1)
+        keep_warm(1)
+        quant_w(0)
+        turn_w(4)
+        keep_warm(1)
+        turn_w(5)
+        keep_warm(1)
+        widen(3, 1)
+        turn_x(2)
+        keep_warm(1)
+        quant_x(0)
+        turn_w(6)
+        keep_warm(1)
+        turn_w(7)
+        keep_warm(1)
+        widen(4, 1)
+        turn_x(3)
+        keep_warm(1)
+        quant_w(1)
+        turn_w(8)
+        keep_warm(1)
+        turn_w(9)
+        keep_warm(1)
+        widen(5, 1)
+        turn_x(4)
+        keep_warm(1)
+        quant_x(1)
+        turn_w(10)
+        keep_warm(1)
+        turn_w(11)
+        keep_warm(1)
+        widen(6, 1)
+        turn_x(5)
+        keep_warm(1)
+        quant_w(2)
+        mm(0, 0)
+        mm(0, 1)
+        turn_x(6)
+        tables()
+        quant_x(2)
+        widen(7, 1)
+        mm(0, 2)
+        mm(1, 0)
+        turn_x(7)
+        mm(1, 1)
+
+        units = [(m, c) for m in range(NM) for c in range(3)]
+        ahead = 5
+        for i, (m, c) in enumerate(units):
+            rope(m, c)
+            if i == 1:
+                quant_x(3)
+            if i + ahead < len(units):
+                mm(units[i + ahead][0], units[i + ahead][1])

@@ -41,8 +41,7 @@ def tile_attention_pa_kernel(tc, x_bytes, x_scale, freqs, wq, wk, wv, out_0, out
         wgp = ctx.enter_context(tc.tile_pool(name="wgp", bufs=2))
         rp = ctx.enter_context(tc.tile_pool(name="rp", bufs=3))
         op = ctx.enter_context(tc.tile_pool(name="op", bufs=3))
-        ptp = ctx.enter_context(tc.psum_pool(name="ptp", bufs=3))
-        accp = ctx.enter_context(tc.psum_pool(name="accp", bufs=5))
+        psp = ctx.enter_context(tc.psum_pool(name="psp", bufs=8))
 
         scl = const.tile([P, D], F32, name="scl")
         s_cols = const.tile([P, NPASS, 4], F32, name="s_cols")
@@ -71,7 +70,7 @@ def tile_attention_pa_kernel(tc, x_bytes, x_scale, freqs, wq, wk, wv, out_0, out
 
         def keep_warm(count):
             for i in range(count):
-                junk = accp.tile([P, 512], F32, name="acc")
+                junk = psp.tile([P, 512], F32, name="bank")
                 nc.tensor.matmul(out=junk[:], lhsT=idle[:, 0:P], rhs=idle[:], start=True, stop=True)
 
         nc.sync.dma_start(out=s_cols[:], in_=sc_d.rearrange("(g p t) -> p g t", p=P, t=4))
@@ -95,7 +94,7 @@ def tile_attention_pa_kernel(tc, x_bytes, x_scale, freqs, wq, wk, wv, out_0, out
         keep_warm(5)
 
         for g in range(NPASS):
-            pb = ptp.tile([P, 4, P], F32, name="pt")
+            pb = psp.tile([P, 4, P], F32, name="bank")
             for t in range(4):
                 nc.tensor.transpose(pb[:, t, :], s_cols[:, g, t:t + 1].to_broadcast([P, P]), ident[:])
             nc.scalar.copy(out=scl[:, 512 * g:512 * (g + 1)].rearrange("p (r t) -> p r t", t=4),
@@ -136,7 +135,7 @@ def tile_attention_pa_kernel(tc, x_bytes, x_scale, freqs, wq, wk, wv, out_0, out
         def turn(src_tile, dst_words):
             words = src_tile[:].bitcast(F32)
             for h in range(2):
-                pt = ptp.tile([P, 2, 2, P], F32, name="pt")
+                pt = psp.tile([P, 2, 2, P], F32, name="bank")
                 for gg in range(2):
                     g = 2 * h + gg
                     for u in range(2):
@@ -171,7 +170,7 @@ def tile_attention_pa_kernel(tc, x_bytes, x_scale, freqs, wq, wk, wv, out_0, out
         acc = {}
 
         def mm(m, c):
-            acc[(m, c)] = accp.tile([P, 512], F32, name="acc")
+            acc[(m, c)] = psp.tile([P, 512], F32, name="bank")
             for g in range(NPASS):
                 nc.tensor.matmul_mx(out=acc[(m, c)][:],
                                     lhsT=xc[m // 2][:, m % 2, P * g:P * (g + 1)].bitcast(FP8X4),
@@ -218,6 +217,10 @@ def tile_attention_pa_kernel(tc, x_bytes, x_scale, freqs, wq, wk, wv, out_0, out
                     add_store(nc.vector, m, 0, 1024)
                 if c == 2:
                     add_store(nc.vector, m, 1024, 1280)
+            elif m == NM - 2:
+                if c == 2:
+                    add_store(nc.gpsimd, m, 0, 1024)
+                    add_store(nc.gpsimd, m, 1024, 1280)
             elif c == 2:
                 add_store(nc.gpsimd, m, 0, 1280)
 
@@ -274,20 +277,23 @@ def tile_attention_pa_kernel(tc, x_bytes, x_scale, freqs, wq, wk, wv, out_0, out
         widen(6, 1)
         turn_x(5)
         keep_warm(1)
-        quant_w(2)
         mm(0, 0)
         mm(0, 1)
+        mm(1, 0)
+        mm(1, 1)
+        quant_w(2)
         turn_x(6)
         tables()
         quant_x(2)
         widen(7, 1)
         mm(0, 2)
-        mm(1, 0)
+        mm(1, 2)
         turn_x(7)
-        mm(1, 1)
+        mm(2, 0)
+        mm(2, 1)
 
         units = [(m, c) for m in range(NM) for c in range(3)]
-        ahead = 5
+        ahead = 8
         for i, (m, c) in enumerate(units):
             rope(m, c)
             if i == 1:

@@ -107,13 +107,14 @@ def tile_attention_pa_kernel(tc, x_bytes, x_scale, freqs, wq, wk, wv, out_0, out
                                 op0=ALU.is_gt, op1=ALU.mult)
         nc.vector.tensor_tensor(out=carg[:], in0=wrap[:], in1=fr[:], op=ALU.subtract)
 
-        def tables():
-            nc.scalar.activation(out=tab[:, :, 0, :].rearrange("p j (i e) -> p j i e", e=2),
-                                 in_=carg[:].unsqueeze(3).to_broadcast([P, 4, 64, 2]),
+        def tables(j0, j1):
+            nj = j1 - j0
+            nc.scalar.activation(out=tab[:, j0:j1, 0, :].rearrange("p j (i e) -> p j i e", e=2),
+                                 in_=carg[:, j0:j1, :].unsqueeze(3).to_broadcast([P, nj, 64, 2]),
                                  func=ACT.Sin, bias=0.5 * math.pi, scale=1.0)
-            tsin = tab[:, :, 1, :].rearrange("p j (i e) -> p j i e", e=2)
-            nc.scalar.activation(out=tsin[:, :, :, 0], in_=fr[:], func=ACT.Sin, bias=math.pi, scale=-1.0)
-            nc.scalar.activation(out=tsin[:, :, :, 1], in_=fr[:], func=ACT.Sin, bias=-math.pi, scale=1.0)
+            tsin = tab[:, j0:j1, 1, :].rearrange("p j (i e) -> p j i e", e=2)
+            nc.scalar.activation(out=tsin[:, :, :, 0], in_=fr[:, j0:j1, :], func=ACT.Sin, bias=math.pi, scale=-1.0)
+            nc.scalar.activation(out=tsin[:, :, :, 1], in_=fr[:, j0:j1, :], func=ACT.Sin, bias=-math.pi, scale=1.0)
 
         xc = [keep.tile([P, 2, 512], U32, name="xc%d" % i, align_bytes=64) for i in range(NM // 2)]
         xsc = [keep.tile([P, 2, 512], U8, name="xsc%d" % i, align_bytes=64) for i in range(NM // 2)]
@@ -267,30 +268,27 @@ def tile_attention_pa_kernel(tc, x_bytes, x_scale, freqs, wq, wk, wv, out_0, out
         turn_w(9)
         keep_warm(1)
         widen(5, 1)
-        turn_x(4)
-        keep_warm(1)
-        quant_x(1)
         turn_w(10)
         keep_warm(1)
         turn_w(11)
         keep_warm(1)
+        quant_x(1)
+        turn_x(4)
+        keep_warm(1)
         widen(6, 1)
         turn_x(5)
         keep_warm(1)
-        mm(0, 0)
-        mm(0, 1)
-        mm(1, 0)
-        mm(1, 1)
+        tables(0, 1)
+        for m, c in ((0, 0), (0, 1), (1, 0), (1, 1)):
+            mm(m, c)
+        widen(7, 1)
         quant_w(2)
         turn_x(6)
-        tables()
-        quant_x(2)
-        widen(7, 1)
-        mm(0, 2)
-        mm(1, 2)
         turn_x(7)
-        mm(2, 0)
-        mm(2, 1)
+        quant_x(2)
+        tables(1, 4)
+        for m, c in ((0, 2), (1, 2), (2, 0), (2, 1)):
+            mm(m, c)
 
         units = [(m, c) for m in range(NM) for c in range(3)]
         ahead = 8

@@ -154,6 +154,40 @@ def tile_attention_pa_kernel(tc, x_bytes, x_scale, freqs, wq, wk, wv, out_0, out
                                   scales=xsc[i][:].rearrange("p a n -> p (a n)"),
                                   in_=xg[i][:].rearrange("p a g r t -> p (a g r t)"))
 
+        planes = const.tile([P, NPASS, 4, P], BF16, name="planes")
+        raw_banks = {}
+
+        def cast_x(m):
+            xs[m] = xsp.tile([P, D], BF16, name="xs", align_bytes=64)
+            nc.scalar.copy(out=xs[m][:], in_=xb[m][:].bitcast(FP8))
+
+        def turn_raw_x(m):
+            words = xs[m][:].bitcast(F32)
+            for h in range(2):
+                raw_banks[h] = psp.tile([P, 2, 2, P], F32, name="bank")
+                for gg in range(2):
+                    g = 2 * h + gg
+                    for u in range(2):
+                        nc.tensor.transpose(raw_banks[h][:, gg, u, :], words[:, 256 * g + u:256 * (g + 1):2], ident[:])
+
+        def scale_out(h):
+            vals = raw_banks[h][:].rearrange("p g u r -> p (g u r)").bitcast(BF16).rearrange(
+                "p (g u r e) -> p g u r e", g=2, u=2, e=2)
+            for gg in range(2):
+                g = 2 * h + gg
+                for u in range(2):
+                    for e in range(2):
+                        t = 2 * u + e
+                        nc.scalar.activation(out=planes[:, g, t, :], in_=vals[:, gg, u, :, e], func=ACT.Copy,
+                                             scale=s_cols[:, g, t:t + 1])
+
+        def weave_x(m):
+            nc.scalar.copy(out=xg[m // 2][:, m % 2, :, :, :], in_=planes[:].rearrange("p g t r -> p g r t"))
+
+        def quant_x_half(m):
+            nc.vector.quantize_mx(out=xc[m // 2][:, m % 2, :].bitcast(FP8X4), scales=xsc[m // 2][:, m % 2, :],
+                                  in_=xg[m // 2][:, m % 2, :, :, :].rearrange("p g r t -> p (g r t)"))
+
         def turn_w(t):
             c, w = t // 4, t % 4
             if w == 0:
@@ -216,12 +250,12 @@ def tile_attention_pa_kernel(tc, x_bytes, x_scale, freqs, wq, wk, wv, out_0, out
             if m == NM - 1:
                 if c == 1:
                     add_store(nc.vector, m, 0, 1024)
+                    add_store(nc.gpsimd, m - 1, 1024, 1280)
                 if c == 2:
                     add_store(nc.vector, m, 1024, 1280)
             elif m == NM - 2:
                 if c == 2:
                     add_store(nc.gpsimd, m, 0, 1024)
-                    add_store(nc.gpsimd, m, 1024, 1280)
             elif c == 2:
                 add_store(nc.gpsimd, m, 0, 1280)
 
@@ -281,20 +315,32 @@ def tile_attention_pa_kernel(tc, x_bytes, x_scale, freqs, wq, wk, wv, out_0, out
         tables(0, 1)
         for m, c in ((0, 0), (0, 1), (1, 0), (1, 1)):
             mm(m, c)
-        widen(7, 1)
         quant_w(2)
         turn_x(6)
-        turn_x(7)
         quant_x(2)
         tables(1, 4)
         for m, c in ((0, 2), (1, 2), (2, 0), (2, 1)):
             mm(m, c)
 
         units = [(m, c) for m in range(NM) for c in range(3)]
-        ahead = 8
+        first_late = 3 * (NM - 1)
         for i, (m, c) in enumerate(units):
             rope(m, c)
             if i == 1:
-                quant_x(3)
-            if i + ahead < len(units):
-                mm(units[i + ahead][0], units[i + ahead][1])
+                quant_x_half(6)
+            if i == 2:
+                cast_x(7)
+            if i == 8:
+                scale_out(0)
+            if i == 11:
+                scale_out(1)
+            if i == 14:
+                weave_x(7)
+            if i == 17:
+                quant_x_half(7)
+            if i + 8 < first_late:
+                mm(units[i + 8][0], units[i + 8][1])
+            if i == 3:
+                turn_raw_x(7)
+            if first_late <= i + 4 < len(units):
+                mm(units[i + 4][0], units[i + 4][1])

@@ -336,7 +336,7 @@ def tile_attention_pa_kernel(tc, x_bytes, x_scale, freqs, wq, wk, wv, out_0, out
                 scale_out(1)
             if i == 14:
                 weave_x(7)
-            if i == 17:
+            if i == 16:
                 quant_x_half(7)
             if i + 8 < first_late:
                 mm(units[i + 8][0], units[i + 8][1])

@@ -188,6 +188,12 @@ def tile_attention_pa_kernel(tc, x_bytes, x_scale, freqs, wq, wk, wv, out_0, out
             nc.vector.quantize_mx(out=xc[m // 2][:, m % 2, :].bitcast(FP8X4), scales=xsc[m // 2][:, m % 2, :],
                                   in_=xg[m // 2][:, m % 2, :, :, :].rearrange("p g r t -> p (g r t)"))
 
+        turnstile = const.tile([P, 1], U32, name="turnstile")
+
+        def quant_last_then_gpsimd():
+            quant_x_half(NM - 1)
+            nc.gpsimd.tensor_copy(out=turnstile[:], in_=xc[(NM - 1) // 2][:, (NM - 1) % 2, 0:1])
+
         def turn_w(t):
             c, w = t // 4, t % 4
             if w == 0:
@@ -229,7 +235,7 @@ def tile_attention_pa_kernel(tc, x_bytes, x_scale, freqs, wq, wk, wv, out_0, out
             if hi > 1024:
                 nc.sync.dma_start(out=k_d[rows, :], in_=oo[m][:, 1024:1280])
 
-        def rope(m, c):
+        def rope(m, c, between=None):
             a = acc[(m, c)]
             j = m % 4
             nh = 4 if c < 2 else 2
@@ -247,6 +253,8 @@ def tile_attention_pa_kernel(tc, x_bytes, x_scale, freqs, wq, wk, wv, out_0, out
                 in0=tab[:, j, :, :].unsqueeze(2).to_broadcast([P, 2, nh, P]),
                 in1=a[:, 0:n].rearrange("p (h c) -> p h c", c=P).unsqueeze(1).to_broadcast([P, 2, nh, P]),
                 op=ALU.mult)
+            if between is not None:
+                between()
             if m == NM - 1:
                 if c == 1:
                     add_store(nc.vector, m, 0, 1024)
@@ -325,7 +333,7 @@ def tile_attention_pa_kernel(tc, x_bytes, x_scale, freqs, wq, wk, wv, out_0, out
         units = [(m, c) for m in range(NM) for c in range(3)]
         first_late = 3 * (NM - 1)
         for i, (m, c) in enumerate(units):
-            rope(m, c)
+            rope(m, c, quant_last_then_gpsimd if i == 17 else None)
             if i == 1:
                 quant_x_half(6)
             if i == 2:
@@ -336,8 +344,6 @@ def tile_attention_pa_kernel(tc, x_bytes, x_scale, freqs, wq, wk, wv, out_0, out
                 scale_out(1)
             if i == 14:
                 weave_x(7)
-            if i == 16:
-                quant_x_half(7)
             if i + 8 < first_late:
                 mm(units[i + 8][0], units[i + 8][1])
             if i == 3:

@@ -65,14 +65,6 @@ def tile_attention_pa_kernel(tc, x_bytes, x_scale, freqs, wq, wk, wv, out_0, out
             nc.sync.dma_start(out=wr[t][:], in_=src)
 
         nc.vector.memset(zero[:], 0.0)
-        idle = const.tile([P, 512], BF16, name="idle")
-        nc.vector.memset(idle[:], 0.0)
-
-        def keep_warm(count):
-            for i in range(count):
-                junk = psp.tile([P, 512], F32, name="bank")
-                nc.tensor.matmul(out=junk[:], lhsT=idle[:, 0:P], rhs=idle[:], start=True, stop=True)
-
         nc.sync.dma_start(out=s_cols[:], in_=sc_d.rearrange("(g p t) -> p g t", p=P, t=4))
         nc.scalar.dma_start(out=fr[:], in_=fr_d)
         nc.scalar.activation(out=warm[:], in_=zero[:], func=ACT.Sin)
@@ -91,7 +83,6 @@ def tile_attention_pa_kernel(tc, x_bytes, x_scale, freqs, wq, wk, wv, out_0, out
 
         ident = const.tile([P, P], F32, name="ident")
         make_identity(nc, ident[:])
-        keep_warm(5)
 
         for g in range(NPASS):
             pb = psp.tile([P, 4, P], F32, name="bank")
@@ -244,15 +235,15 @@ def tile_attention_pa_kernel(tc, x_bytes, x_scale, freqs, wq, wk, wv, out_0, out
             if c == 0:
                 tt[m] = rp.tile([P, 2, 1280], F32, name="t")
                 oo[m] = op.tile([P, 1280], F32, name="o")
-            if c == 2:
-                ov = op.tile([P, 256], F32, name="ov")
-                nc.scalar.copy(out=ov[:], in_=a[:, 256:512])
-                nc.sync.dma_start(out=v_d[rows, :], in_=ov[:])
             nc.vector.tensor_tensor(
                 out=tt[m][:, :, 512 * c:512 * c + n].rearrange("p r (h c) -> p r h c", c=P),
                 in0=tab[:, j, :, :].unsqueeze(2).to_broadcast([P, 2, nh, P]),
                 in1=a[:, 0:n].rearrange("p (h c) -> p h c", c=P).unsqueeze(1).to_broadcast([P, 2, nh, P]),
                 op=ALU.mult)
+            if c == 2:
+                ov = op.tile([P, 256], F32, name="ov")
+                nc.scalar.copy(out=ov[:], in_=a[:, 256:512])
+                nc.sync.dma_start(out=v_d[rows, :], in_=ov[:])
             if between is not None:
                 between()
             if m == NM - 1:
@@ -269,57 +260,39 @@ def tile_attention_pa_kernel(tc, x_bytes, x_scale, freqs, wq, wk, wv, out_0, out
 
         widen(0, 4)
         turn_w(0)
-        keep_warm(1)
         load_w(8)
         turn_w(1)
-        keep_warm(1)
         load_w(9)
         widen(1, 1)
         turn_x(0)
-        keep_warm(1)
         turn_w(2)
-        keep_warm(1)
         load_w(10)
         turn_w(3)
-        keep_warm(1)
         load_w(11)
         load_x(6)
         load_x(7)
         widen(2, 1)
         turn_x(1)
-        keep_warm(1)
         quant_w(0)
         turn_w(4)
-        keep_warm(1)
         turn_w(5)
-        keep_warm(1)
         widen(3, 1)
         turn_x(2)
-        keep_warm(1)
         quant_x(0)
         turn_w(6)
-        keep_warm(1)
         turn_w(7)
-        keep_warm(1)
         widen(4, 1)
         turn_x(3)
-        keep_warm(1)
         quant_w(1)
         turn_w(8)
-        keep_warm(1)
         turn_w(9)
-        keep_warm(1)
         widen(5, 1)
         turn_w(10)
-        keep_warm(1)
         turn_w(11)
-        keep_warm(1)
         quant_x(1)
         turn_x(4)
-        keep_warm(1)
         widen(6, 1)
         turn_x(5)
-        keep_warm(1)
         tables(0, 1)
         for m, c in ((0, 0), (0, 1), (1, 0), (1, 1)):
             mm(m, c)

@@ -65,6 +65,14 @@ def tile_attention_pa_kernel(tc, x_bytes, x_scale, freqs, wq, wk, wv, out_0, out
             nc.sync.dma_start(out=wr[t][:], in_=src)
 
         nc.vector.memset(zero[:], 0.0)
+        idle = const.tile([P, 512], BF16, name="idle")
+        nc.vector.memset(idle[:], 0.0)
+
+        def keep_warm(count):
+            for i in range(count):
+                junk = psp.tile([P, 512], F32, name="bank")
+                nc.tensor.matmul(out=junk[:], lhsT=idle[:, 0:P], rhs=idle[:], start=True, stop=True)
+
         nc.sync.dma_start(out=s_cols[:], in_=sc_d.rearrange("(g p t) -> p g t", p=P, t=4))
         nc.scalar.dma_start(out=fr[:], in_=fr_d)
         nc.scalar.activation(out=warm[:], in_=zero[:], func=ACT.Sin)
@@ -83,6 +91,7 @@ def tile_attention_pa_kernel(tc, x_bytes, x_scale, freqs, wq, wk, wv, out_0, out
 
         ident = const.tile([P, P], F32, name="ident")
         make_identity(nc, ident[:])
+        keep_warm(5)
 
         for g in range(NPASS):
             pb = psp.tile([P, 4, P], F32, name="bank")
@@ -273,26 +282,30 @@ def tile_attention_pa_kernel(tc, x_bytes, x_scale, freqs, wq, wk, wv, out_0, out
         load_x(7)
         widen(2, 1)
         turn_x(1)
+        widen(3, 1)
         quant_w(0)
         turn_w(4)
         turn_w(5)
-        widen(3, 1)
         turn_x(2)
+        widen(4, 1)
         quant_x(0)
         turn_w(6)
         turn_w(7)
-        widen(4, 1)
         turn_x(3)
+        widen(5, 1)
         quant_w(1)
         turn_w(8)
         turn_w(9)
-        widen(5, 1)
         turn_w(10)
+        keep_warm(1)
         turn_w(11)
+        keep_warm(1)
+        widen(6, 1)
         quant_x(1)
         turn_x(4)
-        widen(6, 1)
+        keep_warm(1)
         turn_x(5)
+        keep_warm(1)
         tables(0, 1)
         for m, c in ((0, 0), (0, 1), (1, 0), (1, 1)):
             mm(m, c)

@@ -73,9 +73,10 @@ def tile_attention_pa_kernel(tc, x_bytes, x_scale, freqs, wq, wk, wv, out_0, out
                 junk = psp.tile([P, 512], F32, name="bank")
                 nc.tensor.matmul(out=junk[:], lhsT=idle[:, 0:P], rhs=idle[:], start=True, stop=True)
 
-        nc.sync.dma_start(out=s_cols[:], in_=sc_d.rearrange("(g p t) -> p g t", p=P, t=4))
+        nc.scalar.dma_start(out=s_cols[:], in_=sc_d.rearrange("(g p t) -> p g t", p=P, t=4))
         nc.scalar.dma_start(out=fr[:], in_=fr_d)
         nc.scalar.activation(out=warm[:], in_=zero[:], func=ACT.Sin)
+        load_x(6)
         load_x(0)
         load_w(0)
         load_x(1)
@@ -106,6 +107,8 @@ def tile_attention_pa_kernel(tc, x_bytes, x_scale, freqs, wq, wk, wv, out_0, out
         nc.vector.tensor_scalar(out=wrap[:], in0=fr[:], scalar1=1.5 * math.pi, scalar2=2.0 * math.pi,
                                 op0=ALU.is_gt, op1=ALU.mult)
         nc.vector.tensor_tensor(out=carg[:], in0=wrap[:], in1=fr[:], op=ALU.subtract)
+        xr6 = const.tile([P, D], BF16, name="xr6", align_bytes=64)
+        nc.vector.tensor_copy(out=xr6[:], in_=xb[6][:].bitcast(FP8))
 
         def tables(j0, j1):
             nj = j1 - j0
@@ -154,35 +157,35 @@ def tile_attention_pa_kernel(tc, x_bytes, x_scale, freqs, wq, wk, wv, out_0, out
                                   scales=xsc[i][:].rearrange("p a n -> p (a n)"),
                                   in_=xg[i][:].rearrange("p a g r t -> p (a g r t)"))
 
-        planes = const.tile([P, NPASS, 4, P], BF16, name="planes")
+        planes = const.tile([P, NPASS, 4, 2 * P], BF16, name="planes")
         raw_banks = {}
 
         def cast_x(m):
             xs[m] = xsp.tile([P, D], BF16, name="xs", align_bytes=64)
             nc.scalar.copy(out=xs[m][:], in_=xb[m][:].bitcast(FP8))
 
-        def turn_raw_x(m):
-            words = xs[m][:].bitcast(F32)
-            for h in range(2):
-                raw_banks[h] = psp.tile([P, 2, 2, P], F32, name="bank")
-                for gg in range(2):
-                    g = 2 * h + gg
-                    for u in range(2):
-                        nc.tensor.transpose(raw_banks[h][:, gg, u, :], words[:, 256 * g + u:256 * (g + 1):2], ident[:])
+        def turn_raw(g):
+            raw_banks[g] = psp.tile([P, 2, 2, P], F32, name="bank")
+            for u in range(2):
+                for a in range(2):
+                    src = xr6 if a == 0 else xs[7]
+                    nc.tensor.transpose(raw_banks[g][:, u, a, :],
+                                        src[:].bitcast(F32)[:, 256 * g + u:256 * (g + 1):2], ident[:])
 
-        def scale_out(h):
-            vals = raw_banks[h][:].rearrange("p g u r -> p (g u r)").bitcast(BF16).rearrange(
-                "p (g u r e) -> p g u r e", g=2, u=2, e=2)
-            for gg in range(2):
-                g = 2 * h + gg
-                for u in range(2):
-                    for e in range(2):
-                        t = 2 * u + e
-                        nc.scalar.activation(out=planes[:, g, t, :], in_=vals[:, gg, u, :, e], func=ACT.Copy,
-                                             scale=s_cols[:, g, t:t + 1])
+        def scale_out(g):
+            vals = raw_banks[g][:].rearrange("p u a r -> p (u a r)").bitcast(BF16).rearrange(
+                "p (u n e) -> p u n e", u=2, e=2)
+            for u in range(2):
+                for e in range(2):
+                    t = 2 * u + e
+                    nc.scalar.activation(out=planes[:, g, t, :], in_=vals[:, u, :, e], func=ACT.Copy,
+                                         scale=s_cols[:, g, t:t + 1])
 
-        def weave_x(m):
-            nc.scalar.copy(out=xg[m // 2][:, m % 2, :, :, :], in_=planes[:].rearrange("p g t r -> p g r t"))
+        def weave_x(a):
+            if a == 0:
+                xg[3] = xgp.tile([P, 2, NPASS, P, 4], BF16, name="xg", align_bytes=64)
+            nc.scalar.copy(out=xg[3][:, a, :, :, :],
+                           in_=planes[:, :, :, P * a:P * (a + 1)].rearrange("p g t r -> p g r t"))
 
         def quant_x_half(m):
             nc.vector.quantize_mx(out=xc[m // 2][:, m % 2, :].bitcast(FP8X4), scales=xsc[m // 2][:, m % 2, :],
@@ -190,9 +193,9 @@ def tile_attention_pa_kernel(tc, x_bytes, x_scale, freqs, wq, wk, wv, out_0, out
 
         turnstile = const.tile([P, 1], U32, name="turnstile")
 
-        def quant_last_then_gpsimd():
-            quant_x_half(NM - 1)
-            nc.gpsimd.tensor_copy(out=turnstile[:], in_=xc[(NM - 1) // 2][:, (NM - 1) % 2, 0:1])
+        def quant_then_gpsimd(m):
+            quant_x_half(m)
+            nc.gpsimd.tensor_copy(out=turnstile[:], in_=xc[m // 2][:, m % 2, 0:1])
 
         def turn_w(t):
             c, w = t // 4, t % 4
@@ -278,7 +281,6 @@ def tile_attention_pa_kernel(tc, x_bytes, x_scale, freqs, wq, wk, wv, out_0, out
         load_w(10)
         turn_w(3)
         load_w(11)
-        load_x(6)
         load_x(7)
         widen(2, 1)
         turn_x(1)
@@ -300,39 +302,41 @@ def tile_attention_pa_kernel(tc, x_bytes, x_scale, freqs, wq, wk, wv, out_0, out
         keep_warm(1)
         turn_w(11)
         keep_warm(1)
-        widen(6, 1)
         quant_x(1)
         turn_x(4)
         keep_warm(1)
         turn_x(5)
         keep_warm(1)
         tables(0, 1)
-        for m, c in ((0, 0), (0, 1), (1, 0), (1, 1)):
+        cast_x(7)
+        for m, c in ((0, 0), (0, 1), (1, 0)):
             mm(m, c)
         quant_w(2)
-        turn_x(6)
+        for g in range(NPASS):
+            turn_raw(g)
         quant_x(2)
         tables(1, 4)
-        for m, c in ((0, 2), (1, 2), (2, 0), (2, 1)):
+        scale_out(0)
+        scale_out(1)
+        for m, c in ((0, 2), (1, 1), (1, 2), (2, 0), (2, 1)):
             mm(m, c)
 
         units = [(m, c) for m in range(NM) for c in range(3)]
-        first_late = 3 * (NM - 1)
+        first_late = 3 * (NM - 2)
+        late_quant = {14: 6, 17: 7}
         for i, (m, c) in enumerate(units):
-            rope(m, c, quant_last_then_gpsimd if i == 17 else None)
-            if i == 1:
-                quant_x_half(6)
+            if i in late_quant:
+                rope(m, c, lambda: quant_then_gpsimd(late_quant[i]))
+            else:
+                rope(m, c)
             if i == 2:
-                cast_x(7)
+                scale_out(2)
+                scale_out(3)
+            if i == 5:
+                weave_x(0)
             if i == 8:
-                scale_out(0)
-            if i == 11:
-                scale_out(1)
-            if i == 14:
-                weave_x(7)
+                weave_x(1)
             if i + 8 < first_late:
                 mm(units[i + 8][0], units[i + 8][1])
-            if i == 3:
-                turn_raw_x(7)
             if first_late <= i + 4 < len(units):
                 mm(units[i + 4][0], units[i + 4][1])

import math
from contextlib import ExitStack

import concourse.mybir as mybir
from concourse.masks import make_identity

F32 = mybir.dt.float32
BF16 = mybir.dt.bfloat16
U8 = mybir.dt.uint8
U32 = mybir.dt.uint32
FP8 = mybir.dt.float8_e4m3fn
FP8X4 = mybir.dt.float8_e4m3fn_x4
ACT = mybir.ActivationFunctionType
ALU = mybir.AluOpType

P = 128
TOK = 1024
D = 2048
NPASS = 4
NM = TOK // P
FLOPS = 2 * TOK * D * 1536


def tile_attention_pa_kernel(tc, x_bytes, x_scale, freqs, wq, wk, wv, out_0, out_1, out_2):
    nc = tc.nc
    xb_d = x_bytes.flatten_outer_dims()
    sc_d = x_scale.rearrange("a b c k -> (a b c k)")
    fr_d = freqs.rearrange("s k i -> (s k) i").rearrange("(j p) i -> p j i", p=P)
    q_d = out_0.rearrange("b s k h d -> (b s k) (h d)")
    k_d = out_1.rearrange("b s k h d -> (b s k) (h d)")
    v_d = out_2.rearrange("b s k h d -> (b s k) (h d)")

    with ExitStack() as ctx:
        ctx.enter_context(tc.manual_schedule())
        const = ctx.enter_context(tc.tile_pool(name="const", bufs=1))
        raw = ctx.enter_context(tc.tile_pool(name="raw", bufs=1))
        wrp = ctx.enter_context(tc.tile_pool(name="wrp", bufs=8))
        keep = ctx.enter_context(tc.tile_pool(name="keep", bufs=1))
        xsp = ctx.enter_context(tc.tile_pool(name="xsp", bufs=4))
        xgp = ctx.enter_context(tc.tile_pool(name="xgp", bufs=2))
        wgp = ctx.enter_context(tc.tile_pool(name="wgp", bufs=2))
        rp = ctx.enter_context(tc.tile_pool(name="rp", bufs=3))
        op = ctx.enter_context(tc.tile_pool(name="op", bufs=3))
        psp = ctx.enter_context(tc.psum_pool(name="psp", bufs=8))

        scl = const.tile([P, D], F32, name="scl")
        s_cols = const.tile([P, NPASS, 4], F32, name="s_cols")
        xb = [raw.tile([P, D], U8, name="xb%d" % m) for m in range(NM)]
        wr = {}
        fr = const.tile([P, 4, 64], BF16, name="fr")
        zero = const.tile([P, 1], F32, name="zero")
        warm = const.tile([P, 1], F32, name="warm")

        def load_x(m):
            nc.sync.dma_start(out=xb[m][:], in_=xb_d[P * m:P * (m + 1), :])

        def load_w(t):
            if t < 8:
                src = wq[P * t:P * (t + 1), :]
            elif t < 10:
                src = wk[P * (t - 8):P * (t - 7), :]
            else:
                src = wv[P * (t - 10):P * (t - 9), :]
            wr[t] = wrp.tile([P, D], BF16, name="wr")
            nc.sync.dma_start(out=wr[t][:], in_=src)

        nc.vector.memset(zero[:], 0.0)
        idle = const.tile([P, 512], BF16, name="idle")
        nc.vector.memset(idle[:], 0.0)

        def keep_warm(count):
            for i in range(count):
                junk = psp.tile([P, 512], F32, name="bank")
                nc.tensor.matmul(out=junk[:], lhsT=idle[:, 0:P], rhs=idle[:], start=True, stop=True)

        nc.scalar.dma_start(out=s_cols[:], in_=sc_d.rearrange("(g p t) -> p g t", p=P, t=4))
        nc.scalar.dma_start(out=fr[:], in_=fr_d)
        nc.scalar.activation(out=warm[:], in_=zero[:], func=ACT.Sin)
        load_x(6)
        load_x(0)
        load_w(0)
        load_x(1)
        load_w(1)
        load_w(2)
        load_x(2)
        load_w(3)
        load_x(3)
        for t in range(4, 8):
            load_w(t)
        load_x(4)
        load_x(5)

        ident = const.tile([P, P], F32, name="ident")
        make_identity(nc, ident[:])
        keep_warm(5)

        for g in range(NPASS):
            pb = psp.tile([P, 4, P], F32, name="bank")
            for t in range(4):
                nc.tensor.transpose(pb[:, t, :], s_cols[:, g, t:t + 1].to_broadcast([P, P]), ident[:])
            nc.scalar.copy(out=scl[:, 512 * g:512 * (g + 1)].rearrange("p (r t) -> p r t", t=4),
                           in_=pb[:].rearrange("p t r -> p r t"))

        wrap = const.tile([P, 4, 64], F32, name="wrap")
        carg = const.tile([P, 4, 64], F32, name="carg")
        tab = const.tile([P, 4, 2, P], F32, name="tab")
        nc.vector.tensor_scalar(out=wrap[:], in0=fr[:], scalar1=1.5 * math.pi, scalar2=2.0 * math.pi,
                                op0=ALU.is_gt, op1=ALU.mult)
        nc.vector.tensor_tensor(out=carg[:], in0=wrap[:], in1=fr[:], op=ALU.subtract)
        xr6 = const.tile([P, D], BF16, name="xr6", align_bytes=64)
        nc.vector.tensor_copy(out=xr6[:], in_=xb[6][:].bitcast(FP8))

        def tables(j0, j1):
            nj = j1 - j0
            nc.scalar.activation(out=tab[:, j0:j1, 0, :].rearrange("p j (i e) -> p j i e", e=2),
                                 in_=carg[:, j0:j1, :].unsqueeze(3).to_broadcast([P, nj, 64, 2]),
                                 func=ACT.Sin, bias=0.5 * math.pi, scale=1.0)
            tsin = tab[:, j0:j1, 1, :].rearrange("p j (i e) -> p j i e", e=2)
            nc.scalar.activation(out=tsin[:, :, :, 0], in_=fr[:, j0:j1, :], func=ACT.Sin, bias=math.pi, scale=-1.0)
            nc.scalar.activation(out=tsin[:, :, :, 1], in_=fr[:, j0:j1, :], func=ACT.Sin, bias=-math.pi, scale=1.0)

        xc = [keep.tile([P, 2, 512], U32, name="xc%d" % i, align_bytes=64) for i in range(NM // 2)]
        xsc = [keep.tile([P, 2, 512], U8, name="xsc%d" % i, align_bytes=64) for i in range(NM // 2)]
        wc = [keep.tile([P, NPASS, 512], U32, name="wc%d" % c, align_bytes=64) for c in range(3)]
        wsc = [keep.tile([P, NPASS, 512], U8, name="wsc%d" % c, align_bytes=64) for c in range(3)]

        xs = {}
        xg = {}
        wg = {}

        def widen(m, chunks):
            xs[m] = xsp.tile([P, D], BF16, name="xs", align_bytes=64)
            w = D // chunks
            for i in range(chunks):
                nc.vector.tensor_tensor(out=xs[m][:, w * i:w * (i + 1)],
                                        in0=xb[m][:, w * i:w * (i + 1)].bitcast(FP8),
                                        in1=scl[:, w * i:w * (i + 1)], op=ALU.mult)

        def turn(src_tile, dst_words):
            words = src_tile[:].bitcast(F32)
            for h in range(2):
                pt = psp.tile([P, 2, 2, P], F32, name="bank")
                for gg in range(2):
                    g = 2 * h + gg
                    for u in range(2):
                        nc.tensor.transpose(pt[:, gg, u, :], words[:, 256 * g + u:256 * (g + 1):2], ident[:])
                nc.scalar.copy(out=dst_words(h), in_=pt[:].rearrange("p g u r -> p g r u"))

        def turn_x(m):
            if m % 2 == 0:
                xg[m // 2] = xgp.tile([P, 2, NPASS, P, 4], BF16, name="xg", align_bytes=64)
            xw = xg[m // 2][:, m % 2, :, :, :].bitcast(F32)
            turn(xs[m], lambda h: xw[:, 2 * h:2 * h + 2, :, :])

        def quant_x(i):
            nc.vector.quantize_mx(out=xc[i][:].rearrange("p a n -> p (a n)").bitcast(FP8X4),
                                  scales=xsc[i][:].rearrange("p a n -> p (a n)"),
                                  in_=xg[i][:].rearrange("p a g r t -> p (a g r t)"))

        planes = const.tile([P, NPASS, 4, 2 * P], BF16, name="planes")
        raw_banks = {}

        def cast_x(m):
            xs[m] = xsp.tile([P, D], BF16, name="xs", align_bytes=64)
            nc.scalar.copy(out=xs[m][:], in_=xb[m][:].bitcast(FP8))

        def turn_raw(g):
            raw_banks[g] = psp.tile([P, 2, 2, P], F32, name="bank")
            for u in range(2):
                for a in range(2):
                    src = xr6 if a == 0 else xs[7]
                    nc.tensor.transpose(raw_banks[g][:, u, a, :],
                                        src[:].bitcast(F32)[:, 256 * g + u:256 * (g + 1):2], ident[:])

        def scale_out(g):
            vals = raw_banks[g][:].rearrange("p u a r -> p (u a r)").bitcast(BF16).rearrange(
                "p (u n e) -> p u n e", u=2, e=2)
            for u in range(2):
                for e in range(2):
                    t = 2 * u + e
                    nc.scalar.activation(out=planes[:, g, t, :], in_=vals[:, u, :, e], func=ACT.Copy,
                                         scale=s_cols[:, g, t:t + 1])

        def weave_x(a):
            if a == 0:
                xg[3] = xgp.tile([P, 2, NPASS, P, 4], BF16, name="xg", align_bytes=64)
            nc.scalar.copy(out=xg[3][:, a, :, :, :],
                           in_=planes[:, :, :, P * a:P * (a + 1)].rearrange("p g t r -> p g r t"))

        def quant_x_half(m):
            nc.vector.quantize_mx(out=xc[m // 2][:, m % 2, :].bitcast(FP8X4), scales=xsc[m // 2][:, m % 2, :],
                                  in_=xg[m // 2][:, m % 2, :, :, :].rearrange("p g r t -> p (g r t)"))

        turnstile = const.tile([P, 1], U32, name="turnstile")

        def quant_then_gpsimd(m):
            quant_x_half(m)
            nc.gpsimd.tensor_copy(out=turnstile[:], in_=xc[m // 2][:, m % 2, 0:1])

        def turn_w(t):
            c, w = t // 4, t % 4
            if w == 0:
                wg[c] = wgp.tile([P, NPASS, 512, 4], BF16, name="wg", align_bytes=64)
            ww = wg[c][:].bitcast(F32)
            turn(wr[t], lambda h: ww[:, 2 * h:2 * h + 2, P * w:P * (w + 1), :])

        def quant_w(c):
            for h in range(2):
                gs = slice(2 * h, 2 * h + 2)
                nc.vector.quantize_mx(out=wc[c][:, gs, :].rearrange("p g n -> p (g n)").bitcast(FP8X4),
                                      scales=wsc[c][:, gs, :].rearrange("p g n -> p (g n)"),
                                      in_=wg[c][:, gs, :, :].rearrange("p g n t -> p (g n t)"))

        acc = {}

        def mm(m, c):
            acc[(m, c)] = psp.tile([P, 512], F32, name="bank")
            for g in range(NPASS):
                nc.tensor.matmul_mx(out=acc[(m, c)][:],
                                    lhsT=xc[m // 2][:, m % 2, P * g:P * (g + 1)].bitcast(FP8X4),
                                    lhsT_scale=xsc[m // 2][:, m % 2, P * g:P * (g + 1)],
                                    rhs=wc[c][:, g, :].bitcast(FP8X4),
                                    rhs_scale=wsc[c][:, g, :],
                                    start=(g == 0), stop=(g == NPASS - 1))

        tt = {}
        oo = {}

        def add_store(eng, m, lo, hi):
            rows = slice(P * m, P * (m + 1))
            eng.tensor_tensor(
                out=oo[m][:, lo:hi].rearrange("p (n e) -> p n e", e=2),
                in0=tt[m][:, 0, lo:hi].rearrange("p (n e) -> p n e", e=2),
                in1=tt[m][:, 1, lo:hi].rearrange("p (n e) -> p n e", e=2)[:, :, ::-1],
                op=ALU.add)
            if lo < 1024:
                nc.sync.dma_start(out=q_d[rows, lo:min(hi, 1024)], in_=oo[m][:, lo:min(hi, 1024)])
            if hi > 1024:
                nc.sync.dma_start(out=k_d[rows, :], in_=oo[m][:, 1024:1280])

        def rope(m, c, between=None):
            a = acc[(m, c)]
            j = m % 4
            nh = 4 if c < 2 else 2
            n = nh * P
            rows = slice(P * m, P * (m + 1))
            if c == 0:
                tt[m] = rp.tile([P, 2, 1280], F32, name="t")
                oo[m] = op.tile([P, 1280], F32, name="o")
            nc.vector.tensor_tensor(
                out=tt[m][:, :, 512 * c:512 * c + n].rearrange("p r (h c) -> p r h c", c=P),
                in0=tab[:, j, :, :].unsqueeze(2).to_broadcast([P, 2, nh, P]),
                in1=a[:, 0:n].rearrange("p (h c) -> p h c", c=P).unsqueeze(1).to_broadcast([P, 2, nh, P]),
                op=ALU.mult)
            if c == 2:
                ov = op.tile([P, 256], F32, name="ov")
                nc.scalar.copy(out=ov[:], in_=a[:, 256:512])
                nc.sync.dma_start(out=v_d[rows, :], in_=ov[:])
            if between is not None:
                between()
            if m == NM - 1:
                if c == 1:
                    add_store(nc.vector, m, 0, 1024)
                    add_store(nc.gpsimd, m - 1, 1024, 1280)
                if c == 2:
                    add_store(nc.vector, m, 1024, 1280)
            elif m == NM - 2:
                if c == 2:
                    add_store(nc.gpsimd, m, 0, 1024)
            elif c == 2:
                add_store(nc.gpsimd, m, 0, 1280)

        widen(0, 4)
        turn_w(0)
        load_w(8)
        turn_w(1)
        load_w(9)
        widen(1, 1)
        turn_x(0)
        turn_w(2)
        load_w(10)
        turn_w(3)
        load_w(11)
        load_x(7)
        widen(2, 1)
        turn_x(1)
        widen(3, 1)
        quant_w(0)
        turn_w(4)
        turn_w(5)
        turn_x(2)
        widen(4, 1)
        quant_x(0)
        turn_w(6)
        turn_w(7)
        turn_x(3)
        widen(5, 1)
        quant_w(1)
        turn_w(8)
        turn_w(9)
        turn_w(10)
        keep_warm(1)
        turn_w(11)
        keep_warm(1)
        quant_x(1)
        turn_x(4)
        keep_warm(1)
        turn_x(5)
        keep_warm(1)
        tables(0, 1)
        cast_x(7)
        for m, c in ((0, 0), (0, 1), (1, 0)):
            mm(m, c)
        quant_w(2)
        for g in range(NPASS):
            turn_raw(g)
        quant_x(2)
        tables(1, 4)
        scale_out(0)
        scale_out(1)
        for m, c in ((0, 2), (1, 1), (1, 2), (2, 0), (2, 1)):
            mm(m, c)

        units = [(m, c) for m in range(NM) for c in range(3)]
        first_late = 3 * (NM - 2)
        late_quant = {14: 6, 17: 7}
        for i, (m, c) in enumerate(units):
            if i in late_quant:
                rope(m, c, lambda: quant_then_gpsimd(late_quant[i]))
            else:
                rope(m, c)
            if i == 2:
                scale_out(2)
                scale_out(3)
            if i == 5:
                weave_x(0)
            if i == 8:
                weave_x(1)
            if i + 8 < first_late:
                mm(units[i + 8][0], units[i + 8][1])
            if first_late <= i + 4 < len(units):
                mm(units[i + 4][0], units[i + 4][1])
